import numpy as np
import ml_dtypes

BF16 = ml_dtypes.bfloat16


def bf(x):
    return np.asarray(x, np.float32).astype(BF16)


def f32(x):
    return np.asarray(x, np.float32)


def f64(x):
    return np.asarray(x).astype(np.float64)


def striped(idx):
    return np.tile(idx.reshape(-1, 16).T, (8, 1))


C, V, B, P, K, T, N = 1024, 2048, 2, 128, 6, 256, 1536


def setup_inputs():
    return {"table": f32(np.random.standard_normal((C, V))), "pos": f32(0.5 * np.random.standard_normal((C, P))), "offs": striped(np.random.permutation(np.tile(np.arange(V), 2))[:N])}


def reference(table, pos, offs):
    idx = offs[:16].T.reshape(-1)
    emb = f64(table)[:, idx].reshape(C, K, T)
    return emb.sum(axis=1) / K + np.tile(f64(pos), (1, B))

@@ -1,0 +1,45 @@
+import concourse.mybir as mybir
+
+F32 = mybir.dt.float32
+U16 = mybir.dt.uint16
+ADD = mybir.AluOpType.add
+
+C, V, B, P, K, T, N = 1024, 2048, 2, 128, 6, 256, 1536
+LANES = 128
+BLOCKS = C // LANES
+PIECE = T // 16
+
+
+def tile_bert_kernel(tc, table, pos, offs, out):
+    nc = tc.nc
+    with (
+        tc.tile_pool(name="held", bufs=1) as held,
+        tc.tile_pool(name="windows", bufs=BLOCKS) as windows,
+        tc.tile_pool(name="work", bufs=3) as work,
+        tc.tile_pool(name="sums", bufs=4) as sums,
+    ):
+        offsets = held.tile([LANES, N // 16], U16, name="offsets")
+        nc.sync.dma_start(offsets[:], offs)
+
+        for c in range(BLOCKS):
+            rows = slice(c * LANES, (c + 1) * LANES)
+            window = windows.tile([LANES, V], F32)
+            nc.sync.dma_start(window[:], table[rows, :])
+            position = work.tile([LANES, P], F32)
+            nc.scalar.dma_start(position[:], pos[rows, :])
+
+            total = sums.tile([LANES, T], F32, name="total")
+            nc.scalar.mul(
+                total[:].rearrange("c (b p) -> c b p", b=B),
+                position[:].unsqueeze(1).to_broadcast([LANES, B, P]),
+                float(K),
+            )
+            for k in range(K):
+                picked = window[:].indirect(offsets[:, k * PIECE : (k + 1) * PIECE])
+                longer = sums.tile([LANES, T], F32, name="total")
+                nc.vector.tensor_tensor(longer[:], picked, total[:], ADD)
+                total = longer
+
+            mean = work.tile([LANES, T], F32)
+            nc.scalar.mul(mean[:], total[:], 1.0 / K)
+            nc.sync.dma_start(out[rows, :], mean[:])

@@ -8,6 +8,7 @@ C, V, B, P, K, T, N = 1024, 2048, 2, 128, 6, 256, 1536
 LANES = 128
 BLOCKS = C // LANES
 PIECE = T // 16
+HALF = K // 2
 
 
 def tile_bert_kernel(tc, table, pos, offs, out):
@@ -16,30 +17,48 @@ def tile_bert_kernel(tc, table, pos, offs, out):
         tc.tile_pool(name="held", bufs=1) as held,
         tc.tile_pool(name="windows", bufs=BLOCKS) as windows,
         tc.tile_pool(name="work", bufs=3) as work,
-        tc.tile_pool(name="sums", bufs=4) as sums,
+        tc.tile_pool(name="sums", bufs=6) as sums,
     ):
         offsets = held.tile([LANES, N // 16], U16, name="offsets")
         nc.sync.dma_start(offsets[:], offs)
 
-        for c in range(BLOCKS):
+        window = {}
+        total = {}
+
+        def begin(c):
             rows = slice(c * LANES, (c + 1) * LANES)
-            window = windows.tile([LANES, V], F32)
-            nc.sync.dma_start(window[:], table[rows, :])
+            window[c] = windows.tile([LANES, V], F32, name="window")
+            nc.sync.dma_start(window[c][:], table[rows, :])
             position = work.tile([LANES, P], F32)
             nc.scalar.dma_start(position[:], pos[rows, :])
-
-            total = sums.tile([LANES, T], F32, name="total")
+            total[c] = sums.tile([LANES, T], F32, name="total")
             nc.scalar.mul(
-                total[:].rearrange("c (b p) -> c b p", b=B),
+                total[c][:].rearrange("c (b p) -> c b p", b=B),
                 position[:].unsqueeze(1).to_broadcast([LANES, B, P]),
                 float(K),
             )
-            for k in range(K):
-                picked = window[:].indirect(offsets[:, k * PIECE : (k + 1) * PIECE])
-                longer = sums.tile([LANES, T], F32, name="total")
-                nc.vector.tensor_tensor(longer[:], picked, total[:], ADD)
-                total = longer
 
+        def add_slot(c, k):
+            picked = window[c][:].indirect(offsets[:, k * PIECE : (k + 1) * PIECE])
+            longer = sums.tile([LANES, T], F32, name="total")
+            nc.vector.tensor_tensor(longer[:], picked, total[c][:], ADD)
+            total[c] = longer
+
+        def finish(c):
+            rows = slice(c * LANES, (c + 1) * LANES)
             mean = work.tile([LANES, T], F32)
-            nc.scalar.mul(mean[:], total[:], 1.0 / K)
+            nc.scalar.mul(mean[:], total[c][:], 1.0 / K)
             nc.sync.dma_start(out[rows, :], mean[:])
+
+        begin(0)
+        for k in range(HALF):
+            add_slot(0, k)
+        for c in range(1, BLOCKS):
+            begin(c)
+            for k in range(HALF):
+                add_slot(c - 1, HALF + k)
+                add_slot(c, k)
+            finish(c - 1)
+        for k in range(HALF):
+            add_slot(BLOCKS - 1, HALF + k)
+        finish(BLOCKS - 1)

@@ -1,3 +1,4 @@
+import concourse.masks as masks
 import concourse.mybir as mybir
 
 F32 = mybir.dt.float32
@@ -5,10 +6,11 @@ U16 = mybir.dt.uint16
 ADD = mybir.AluOpType.add
 
 C, V, B, P, K, T, N = 1024, 2048, 2, 128, 6, 256, 1536
+FLOPS = C * T * (K + 1)
 LANES = 128
 BLOCKS = C // LANES
-PIECE = T // 16
-HALF = K // 2
+FOLD = K // 2
+PIECE = FOLD * T // 16
 
 
 def tile_bert_kernel(tc, table, pos, offs, out):
@@ -17,13 +19,15 @@ def tile_bert_kernel(tc, table, pos, offs, out):
         tc.tile_pool(name="held", bufs=1) as held,
         tc.tile_pool(name="windows", bufs=BLOCKS) as windows,
         tc.tile_pool(name="work", bufs=3) as work,
-        tc.tile_pool(name="sums", bufs=6) as sums,
+        tc.psum_pool(name="banks", bufs=2) as banks,
     ):
         offsets = held.tile([LANES, N // 16], U16, name="offsets")
         nc.sync.dma_start(offsets[:], offs)
+        identity = held.tile([LANES, LANES], F32, name="identity")
+        masks.make_identity(nc, identity[:])
 
         window = {}
-        total = {}
+        wide = {}
 
         def begin(c):
             rows = slice(c * LANES, (c + 1) * LANES)
@@ -31,34 +35,37 @@ def tile_bert_kernel(tc, table, pos, offs, out):
             nc.sync.dma_start(window[c][:], table[rows, :])
             position = work.tile([LANES, P], F32)
             nc.scalar.dma_start(position[:], pos[rows, :])
-            total[c] = sums.tile([LANES, T], F32, name="total")
+            wide[c] = work.tile([LANES, FOLD * T], F32, name="share")
             nc.scalar.mul(
-                total[c][:].rearrange("c (b p) -> c b p", b=B),
-                position[:].unsqueeze(1).to_broadcast([LANES, B, P]),
-                float(K),
+                wide[c][:].rearrange("c (s p) -> c s p", p=P),
+                position[:].unsqueeze(1).to_broadcast([LANES, FOLD * B, P]),
+                float(K // FOLD),
             )
 
-        def add_slot(c, k):
-            picked = window[c][:].indirect(offsets[:, k * PIECE : (k + 1) * PIECE])
-            longer = sums.tile([LANES, T], F32, name="total")
-            nc.vector.tensor_tensor(longer[:], picked, total[c][:], ADD)
-            total[c] = longer
+        def add_slots(c, h):
+            picked = window[c][:].indirect(offsets[:, h * PIECE : (h + 1) * PIECE])
+            longer = work.tile([LANES, FOLD * T], F32, name="wide")
+            nc.vector.tensor_tensor(longer[:], picked, wide[c][:], ADD)
+            wide[c] = longer
 
         def finish(c):
             rows = slice(c * LANES, (c + 1) * LANES)
+            bank = banks.tile([LANES, T], F32)
+            for s in range(FOLD):
+                nc.tensor.matmul(
+                    bank[:], identity[:], wide[c][:, s * T : (s + 1) * T],
+                    start=(s == 0), stop=(s == FOLD - 1),
+                )
             mean = work.tile([LANES, T], F32)
-            nc.scalar.mul(mean[:], total[c][:], 1.0 / K)
+            nc.scalar.mul(mean[:], bank[:], 1.0 / K)
             nc.sync.dma_start(out[rows, :], mean[:])
 
         begin(0)
-        for k in range(HALF):
-            add_slot(0, k)
+        add_slots(0, 0)
         for c in range(1, BLOCKS):
             begin(c)
-            for k in range(HALF):
-                add_slot(c - 1, HALF + k)
-                add_slot(c, k)
+            add_slots(c, 0)
+            add_slots(c - 1, 1)
             finish(c - 1)
-        for k in range(HALF):
-            add_slot(BLOCKS - 1, HALF + k)
+        add_slots(BLOCKS - 1, 1)
         finish(BLOCKS - 1)

@@ -1,4 +1,3 @@
-import concourse.masks as masks
 import concourse.mybir as mybir
 
 F32 = mybir.dt.float32
@@ -6,11 +5,10 @@ U16 = mybir.dt.uint16
 ADD = mybir.AluOpType.add
 
 C, V, B, P, K, T, N = 1024, 2048, 2, 128, 6, 256, 1536
-FLOPS = C * T * (K + 1)
 LANES = 128
 BLOCKS = C // LANES
-FOLD = K // 2
-PIECE = FOLD * T // 16
+PIECE = T // 16
+HALF = K // 2
 
 
 def tile_bert_kernel(tc, table, pos, offs, out):
@@ -19,15 +17,13 @@ def tile_bert_kernel(tc, table, pos, offs, out):
         tc.tile_pool(name="held", bufs=1) as held,
         tc.tile_pool(name="windows", bufs=BLOCKS) as windows,
         tc.tile_pool(name="work", bufs=3) as work,
-        tc.psum_pool(name="banks", bufs=2) as banks,
+        tc.tile_pool(name="sums", bufs=6) as sums,
     ):
         offsets = held.tile([LANES, N // 16], U16, name="offsets")
         nc.sync.dma_start(offsets[:], offs)
-        identity = held.tile([LANES, LANES], F32, name="identity")
-        masks.make_identity(nc, identity[:])
 
         window = {}
-        wide = {}
+        total = {}
 
         def begin(c):
             rows = slice(c * LANES, (c + 1) * LANES)
@@ -35,37 +31,34 @@ def tile_bert_kernel(tc, table, pos, offs, out):
             nc.sync.dma_start(window[c][:], table[rows, :])
             position = work.tile([LANES, P], F32)
             nc.scalar.dma_start(position[:], pos[rows, :])
-            wide[c] = work.tile([LANES, FOLD * T], F32, name="share")
+            total[c] = sums.tile([LANES, T], F32, name="total")
             nc.scalar.mul(
-                wide[c][:].rearrange("c (s p) -> c s p", p=P),
-                position[:].unsqueeze(1).to_broadcast([LANES, FOLD * B, P]),
-                float(K // FOLD),
+                total[c][:].rearrange("c (b p) -> c b p", b=B),
+                position[:].unsqueeze(1).to_broadcast([LANES, B, P]),
+                float(K),
             )
 
-        def add_slots(c, h):
-            picked = window[c][:].indirect(offsets[:, h * PIECE : (h + 1) * PIECE])
-            longer = work.tile([LANES, FOLD * T], F32, name="wide")
-            nc.vector.tensor_tensor(longer[:], picked, wide[c][:], ADD)
-            wide[c] = longer
+        def add_slot(c, k):
+            picked = window[c][:].indirect(offsets[:, k * PIECE : (k + 1) * PIECE])
+            longer = sums.tile([LANES, T], F32, name="total")
+            nc.vector.tensor_tensor(longer[:], picked, total[c][:], ADD)
+            total[c] = longer
 
         def finish(c):
             rows = slice(c * LANES, (c + 1) * LANES)
-            bank = banks.tile([LANES, T], F32)
-            for s in range(FOLD):
-                nc.tensor.matmul(
-                    bank[:], identity[:], wide[c][:, s * T : (s + 1) * T],
-                    start=(s == 0), stop=(s == FOLD - 1),
-                )
             mean = work.tile([LANES, T], F32)
-            nc.scalar.mul(mean[:], bank[:], 1.0 / K)
+            nc.scalar.mul(mean[:], total[c][:], 1.0 / K)
             nc.sync.dma_start(out[rows, :], mean[:])
 
         begin(0)
-        add_slots(0, 0)
+        for k in range(HALF):
+            add_slot(0, k)
         for c in range(1, BLOCKS):
             begin(c)
-            add_slots(c, 0)
-            add_slots(c - 1, 1)
+            for k in range(HALF):
+                add_slot(c, k)
+                add_slot(c - 1, HALF + k)
             finish(c - 1)
-        add_slots(BLOCKS - 1, 1)
+        for k in range(HALF):
+            add_slot(BLOCKS - 1, HALF + k)
         finish(BLOCKS - 1)

@@ -1,4 +1,5 @@
 import concourse.mybir as mybir
+from concourse.masks import make_identity
 
 F32 = mybir.dt.float32
 U16 = mybir.dt.uint16
@@ -7,8 +8,9 @@ ADD = mybir.AluOpType.add
 C, V, B, P, K, T, N = 1024, 2048, 2, 128, 6, 256, 1536
 LANES = 128
 BLOCKS = C // LANES
-PIECE = T // 16
-HALF = K // 2
+HALF = N // 2
+PARTS = HALF // T
+FLOPS = C * T * (K + 1)
 
 
 def tile_bert_kernel(tc, table, pos, offs, out):
@@ -16,49 +18,69 @@ def tile_bert_kernel(tc, table, pos, offs, out):
     with (
         tc.tile_pool(name="held", bufs=1) as held,
         tc.tile_pool(name="windows", bufs=BLOCKS) as windows,
-        tc.tile_pool(name="work", bufs=3) as work,
-        tc.tile_pool(name="sums", bufs=6) as sums,
+        tc.tile_pool(name="work", bufs=4) as work,
+        tc.psum_pool(name="folds", bufs=2) as folds,
     ):
         offsets = held.tile([LANES, N // 16], U16, name="offsets")
         nc.sync.dma_start(offsets[:], offs)
+        identity = held.tile([LANES, LANES], F32, name="identity")
+        make_identity(nc, identity[:])
 
         window = {}
-        total = {}
+        position = {}
+        doubled = {}
 
-        def begin(c):
-            rows = slice(c * LANES, (c + 1) * LANES)
-            window[c] = windows.tile([LANES, V], F32, name="window")
-            nc.sync.dma_start(window[c][:], table[rows, :])
-            position = work.tile([LANES, P], F32)
-            nc.scalar.dma_start(position[:], pos[rows, :])
-            total[c] = sums.tile([LANES, T], F32, name="total")
+        def rows(c):
+            return slice(c * LANES, (c + 1) * LANES)
+
+        def fetch(c):
+            position[c] = work.tile([LANES, P], F32, name="position")
+            nc.scalar.dma_start(position[c][:], pos[rows(c), :])
+
+        def spread(c):
+            doubled[c] = work.tile([LANES, HALF], F32, name="doubled")
             nc.scalar.mul(
-                total[c][:].rearrange("c (b p) -> c b p", b=B),
-                position[:].unsqueeze(1).to_broadcast([LANES, B, P]),
-                float(K),
+                doubled[c][:].rearrange("c (r p) -> c r p", p=P),
+                position[c][:].unsqueeze(1).to_broadcast([LANES, HALF // P, P]),
+                float(K // PARTS),
             )
 
-        def add_slot(c, k):
-            picked = window[c][:].indirect(offsets[:, k * PIECE : (k + 1) * PIECE])
-            longer = sums.tile([LANES, T], F32, name="total")
-            nc.vector.tensor_tensor(longer[:], picked, total[c][:], ADD)
-            total[c] = longer
+        def gather_add(c, half, pieces, other):
+            result = work.tile([LANES, HALF], F32, name="sum%d" % half)
+            width = HALF // pieces
+            for j in range(pieces):
+                cols = slice(j * width, (j + 1) * width)
+                entry = half * HALF + j * width
+                picked = window[c][:].indirect(offsets[:, entry // 16 : (entry + width) // 16])
+                nc.vector.tensor_tensor(result[:, cols], picked, other[:, cols], ADD)
+            return result
 
-        def finish(c):
-            rows = slice(c * LANES, (c + 1) * LANES)
+        def block(c, last_pieces):
+            lower = gather_add(c, 0, 2, doubled[c])
+            both = gather_add(c, 1, last_pieces, lower)
+            total = folds.tile([LANES, T], F32)
+            for j in range(PARTS):
+                nc.tensor.matmul(
+                    total[:],
+                    identity[:],
+                    both[:, j * T : (j + 1) * T],
+                    start=(j == 0),
+                    stop=(j == PARTS - 1),
+                )
             mean = work.tile([LANES, T], F32)
-            nc.scalar.mul(mean[:], total[c][:], 1.0 / K)
-            nc.sync.dma_start(out[rows, :], mean[:])
+            nc.scalar.mul(mean[:], total[:], 1.0 / K)
+            nc.sync.dma_start(out[rows(c), :], mean[:])
 
-        begin(0)
-        for k in range(HALF):
-            add_slot(0, k)
-        for c in range(1, BLOCKS):
-            begin(c)
-            for k in range(HALF):
-                add_slot(c, k)
-                add_slot(c - 1, HALF + k)
-            finish(c - 1)
-        for k in range(HALF):
-            add_slot(BLOCKS - 1, HALF + k)
-        finish(BLOCKS - 1)
+        for c in range(BLOCKS):
+            window[c] = windows.tile([LANES, V], F32, name="window")
+            nc.sync.dma_start(window[c][:], table[rows(c), :])
+
+        fetch(0)
+        fetch(1)
+        spread(0)
+        for c in range(BLOCKS):
+            if c + 2 < BLOCKS:
+                fetch(c + 2)
+            if c + 1 < BLOCKS:
+                spread(c + 1)
+            block(c, 2 if c + 1 < BLOCKS else PARTS)

@@ -28,45 +28,39 @@ def tile_bert_kernel(tc, table, pos, offs, out):
 
         window = {}
         position = {}
-        doubled = {}
+        start = {}
 
         def rows(c):
             return slice(c * LANES, (c + 1) * LANES)
+
+        def width_of(c):
+            return HALF if c + 1 < BLOCKS else T
 
         def fetch(c):
             position[c] = work.tile([LANES, P], F32, name="position")
             nc.scalar.dma_start(position[c][:], pos[rows(c), :])
 
         def spread(c):
-            doubled[c] = work.tile([LANES, HALF], F32, name="doubled")
+            width = width_of(c)
+            start[c] = work.tile([LANES, width], F32, name="start%d" % width)
             nc.scalar.mul(
-                doubled[c][:].rearrange("c (r p) -> c r p", p=P),
-                position[c][:].unsqueeze(1).to_broadcast([LANES, HALF // P, P]),
-                float(K // PARTS),
+                start[c][:].rearrange("c (r p) -> c r p", p=P),
+                position[c][:].unsqueeze(1).to_broadcast([LANES, width // P, P]),
+                float(K * T // width),
             )
 
-        def gather_add(c, half, pieces, other):
-            result = work.tile([LANES, HALF], F32, name="sum%d" % half)
-            width = HALF // pieces
-            for j in range(pieces):
-                cols = slice(j * width, (j + 1) * width)
-                entry = half * HALF + j * width
-                picked = window[c][:].indirect(offsets[:, entry // 16 : (entry + width) // 16])
+        def gather_add(c, entry, other):
+            width = width_of(c)
+            result = work.tile([LANES, width], F32, name="sum%d" % width)
+            piece = width // 2
+            for j in range(2):
+                cols = slice(j * piece, (j + 1) * piece)
+                first = (entry + j * piece) // 16
+                picked = window[c][:].indirect(offsets[:, first : first + piece // 16])
                 nc.vector.tensor_tensor(result[:, cols], picked, other[:, cols], ADD)
             return result
 
-        def block(c, last_pieces):
-            lower = gather_add(c, 0, 2, doubled[c])
-            both = gather_add(c, 1, last_pieces, lower)
-            total = folds.tile([LANES, T], F32)
-            for j in range(PARTS):
-                nc.tensor.matmul(
-                    total[:],
-                    identity[:],
-                    both[:, j * T : (j + 1) * T],
-                    start=(j == 0),
-                    stop=(j == PARTS - 1),
-                )
+        def store_mean(c, total):
             mean = work.tile([LANES, T], F32)
             nc.scalar.mul(mean[:], total[:], 1.0 / K)
             nc.sync.dma_start(out[rows(c), :], mean[:])
@@ -83,4 +77,19 @@ def tile_bert_kernel(tc, table, pos, offs, out):
                 fetch(c + 2)
             if c + 1 < BLOCKS:
                 spread(c + 1)
-            block(c, 2 if c + 1 < BLOCKS else PARTS)
+            running = start[c]
+            for entry in range(0, N, width_of(c)):
+                running = gather_add(c, entry, running)
+            if width_of(c) == T:
+                store_mean(c, running)
+            else:
+                total = folds.tile([LANES, T], F32)
+                for j in range(PARTS):
+                    nc.tensor.matmul(
+                        total[:],
+                        identity[:],
+                        running[:, j * T : (j + 1) * T],
+                        start=(j == 0),
+                        stop=(j == PARTS - 1),
+                    )
+                store_mean(c, total)

@@ -9,7 +9,7 @@ C, V, B, P, K, T, N = 1024, 2048, 2, 128, 6, 256, 1536
 LANES = 128
 BLOCKS = C // LANES
 HALF = N // 2
-PARTS = HALF // T
+AHEAD = 3
 FLOPS = C * T * (K + 1)
 
 
@@ -17,79 +17,78 @@ def tile_bert_kernel(tc, table, pos, offs, out):
     nc = tc.nc
     with (
         tc.tile_pool(name="held", bufs=1) as held,
-        tc.tile_pool(name="windows", bufs=BLOCKS) as windows,
+        tc.tile_pool(name="blocks", bufs=BLOCKS) as blocks,
         tc.tile_pool(name="work", bufs=4) as work,
-        tc.psum_pool(name="folds", bufs=2) as folds,
+        tc.psum_pool(name="folds", bufs=4) as folds,
     ):
         offsets = held.tile([LANES, N // 16], U16, name="offsets")
         nc.sync.dma_start(offsets[:], offs)
         identity = held.tile([LANES, LANES], F32, name="identity")
         make_identity(nc, identity[:])
 
-        window = {}
-        position = {}
-        start = {}
-
         def rows(c):
             return slice(c * LANES, (c + 1) * LANES)
 
-        def width_of(c):
-            return HALF if c + 1 < BLOCKS else T
+        window = {}
+        position = {}
+        repeated = {}
+        for c in range(BLOCKS):
+            window[c] = blocks.tile([LANES, V], F32, name="window")
+            nc.sync.dma_start(window[c][:], table[rows(c), :])
 
         def fetch(c):
-            position[c] = work.tile([LANES, P], F32, name="position")
+            position[c] = blocks.tile([LANES, P], F32, name="position")
             nc.scalar.dma_start(position[c][:], pos[rows(c), :])
 
         def spread(c):
-            width = width_of(c)
-            start[c] = work.tile([LANES, width], F32, name="start%d" % width)
-            nc.scalar.mul(
-                start[c][:].rearrange("c (r p) -> c r p", p=P),
-                position[c][:].unsqueeze(1).to_broadcast([LANES, width // P, P]),
-                float(K * T // width),
+            repeated[c] = work.tile([LANES, HALF], F32, name="repeated")
+            nc.scalar.copy(
+                repeated[c][:].rearrange("c (r p) -> c r p", p=P),
+                position[c][:].unsqueeze(1).to_broadcast([LANES, HALF // P, P]),
             )
 
-        def gather_add(c, entry, other):
-            width = width_of(c)
-            result = work.tile([LANES, width], F32, name="sum%d" % width)
-            piece = width // 2
-            for j in range(2):
-                cols = slice(j * piece, (j + 1) * piece)
-                first = (entry + j * piece) // 16
-                picked = window[c][:].indirect(offsets[:, first : first + piece // 16])
-                nc.vector.tensor_tensor(result[:, cols], picked, other[:, cols], ADD)
-            return result
+        for c in range(AHEAD):
+            fetch(c)
+        spread(0)
 
         def store_mean(c, total):
             mean = work.tile([LANES, T], F32)
             nc.scalar.mul(mean[:], total[:], 1.0 / K)
             nc.sync.dma_start(out[rows(c), :], mean[:])
 
-        for c in range(BLOCKS):
-            window[c] = windows.tile([LANES, V], F32, name="window")
-            nc.sync.dma_start(window[c][:], table[rows(c), :])
-
-        fetch(0)
-        fetch(1)
-        spread(0)
-        for c in range(BLOCKS):
-            if c + 2 < BLOCKS:
-                fetch(c + 2)
-            if c + 1 < BLOCKS:
+        for c in range(BLOCKS - 1):
+            if c + AHEAD < BLOCKS:
+                fetch(c + AHEAD)
+            if c + 1 < BLOCKS - 1:
                 spread(c + 1)
-            running = start[c]
-            for entry in range(0, N, width_of(c)):
-                running = gather_add(c, entry, running)
-            if width_of(c) == T:
-                store_mean(c, running)
-            else:
-                total = folds.tile([LANES, T], F32)
-                for j in range(PARTS):
-                    nc.tensor.matmul(
-                        total[:],
-                        identity[:],
-                        running[:, j * T : (j + 1) * T],
-                        start=(j == 0),
-                        stop=(j == PARTS - 1),
-                    )
-                store_mean(c, total)
+            terms = work.tile([LANES, N], F32)
+            for h in range(2):
+                picked = window[c][:].indirect(
+                    offsets[:, h * HALF // 16 : (h + 1) * HALF // 16]
+                )
+                nc.vector.tensor_tensor(
+                    terms[:, h * HALF : (h + 1) * HALF], picked, repeated[c][:], ADD
+                )
+            total = folds.tile([LANES, T], F32)
+            for k in range(K):
+                nc.tensor.matmul(
+                    total[:],
+                    identity[:],
+                    terms[:, k * T : (k + 1) * T],
+                    start=(k == 0),
+                    stop=(k == K - 1),
+                )
+            store_mean(c, total)
+
+        last = BLOCKS - 1
+        sixfold = work.tile([LANES, P], F32)
+        nc.scalar.mul(sixfold[:], position[last][:], float(K))
+        running = [sixfold[:], sixfold[:]]
+        for k in range(K):
+            longer = work.tile([LANES, T], F32)
+            for b in range(B):
+                first = (k * T + b * P) // 16
+                picked = window[last][:].indirect(offsets[:, first : first + P // 16])
+                nc.vector.tensor_tensor(longer[:, b * P : (b + 1) * P], picked, running[b], ADD)
+            running = [longer[:, b * P : (b + 1) * P] for b in range(B)]
+        store_mean(last, longer)

@@ -8,7 +8,6 @@ ADD = mybir.AluOpType.add
 C, V, B, P, K, T, N = 1024, 2048, 2, 128, 6, 256, 1536
 LANES = 128
 BLOCKS = C // LANES
-HALF = N // 2
 AHEAD = 3
 FLOPS = C * T * (K + 1)
 
@@ -41,10 +40,10 @@ def tile_bert_kernel(tc, table, pos, offs, out):
             nc.scalar.dma_start(position[c][:], pos[rows(c), :])
 
         def spread(c):
-            repeated[c] = work.tile([LANES, HALF], F32, name="repeated")
+            repeated[c] = work.tile([LANES, N], F32, name="repeated")
             nc.scalar.copy(
                 repeated[c][:].rearrange("c (r p) -> c r p", p=P),
-                position[c][:].unsqueeze(1).to_broadcast([LANES, HALF // P, P]),
+                position[c][:].unsqueeze(1).to_broadcast([LANES, N // P, P]),
             )
 
         for c in range(AHEAD):
@@ -62,13 +61,9 @@ def tile_bert_kernel(tc, table, pos, offs, out):
             if c + 1 < BLOCKS - 1:
                 spread(c + 1)
             terms = work.tile([LANES, N], F32)
-            for h in range(2):
-                picked = window[c][:].indirect(
-                    offsets[:, h * HALF // 16 : (h + 1) * HALF // 16]
-                )
-                nc.vector.tensor_tensor(
-                    terms[:, h * HALF : (h + 1) * HALF], picked, repeated[c][:], ADD
-                )
+            nc.vector.tensor_tensor(
+                terms[:], window[c][:].indirect(offsets[:]), repeated[c][:], ADD
+            )
             total = folds.tile([LANES, T], F32)
             for k in range(K):
                 nc.tensor.matmul(

@@ -8,6 +8,8 @@ ADD = mybir.AluOpType.add
 C, V, B, P, K, T, N = 1024, 2048, 2, 128, 6, 256, 1536
 LANES = 128
 BLOCKS = C // LANES
+CHAINED = 2
+WIDE = BLOCKS - CHAINED
 AHEAD = 3
 FLOPS = C * T * (K + 1)
 
@@ -55,11 +57,24 @@ def tile_bert_kernel(tc, table, pos, offs, out):
             nc.scalar.mul(mean[:], total[:], 1.0 / K)
             nc.sync.dma_start(out[rows(c), :], mean[:])
 
-        for c in range(BLOCKS - 1):
+        running = {}
+
+        def seed(c):
+            running[c] = work.tile([LANES, T], F32, name="sixfold")
+            nc.scalar.mul(
+                running[c][:].rearrange("c (b p) -> c b p", p=P),
+                position[c][:].unsqueeze(1).to_broadcast([LANES, B, P]),
+                float(K),
+            )
+
+        for c in range(WIDE):
             if c + AHEAD < BLOCKS:
                 fetch(c + AHEAD)
-            if c + 1 < BLOCKS - 1:
+            if c + 1 < WIDE:
                 spread(c + 1)
+            else:
+                for d in range(WIDE, BLOCKS):
+                    seed(d)
             terms = work.tile([LANES, N], F32)
             nc.vector.tensor_tensor(
                 terms[:], window[c][:].indirect(offsets[:]), repeated[c][:], ADD
@@ -75,15 +90,11 @@ def tile_bert_kernel(tc, table, pos, offs, out):
                 )
             store_mean(c, total)
 
-        last = BLOCKS - 1
-        sixfold = work.tile([LANES, P], F32)
-        nc.scalar.mul(sixfold[:], position[last][:], float(K))
-        running = [sixfold[:], sixfold[:]]
         for k in range(K):
-            longer = work.tile([LANES, T], F32)
-            for b in range(B):
-                first = (k * T + b * P) // 16
-                picked = window[last][:].indirect(offsets[:, first : first + P // 16])
-                nc.vector.tensor_tensor(longer[:, b * P : (b + 1) * P], picked, running[b], ADD)
-            running = [longer[:, b * P : (b + 1) * P] for b in range(B)]
-        store_mean(last, longer)
+            for c in range(WIDE, BLOCKS):
+                longer = work.tile([LANES, T], F32)
+                picked = window[c][:].indirect(offsets[:, k * T // 16 : (k + 1) * T // 16])
+                nc.vector.tensor_tensor(longer[:], picked, running[c][:], ADD)
+                running[c] = longer
+        for c in range(WIDE, BLOCKS):
+            store_mean(c, running[c])

@@ -41,11 +41,15 @@ def tile_bert_kernel(tc, table, pos, offs, out):
             position[c] = blocks.tile([LANES, P], F32, name="position")
             nc.scalar.dma_start(position[c][:], pos[rows(c), :])
 
+        def pieces(c):
+            return 2 if c == 0 else 1
+
         def spread(c):
-            repeated[c] = work.tile([LANES, N], F32, name="repeated")
+            width = N // pieces(c)
+            repeated[c] = work.tile([LANES, width], F32, name="repeated")
             nc.scalar.copy(
                 repeated[c][:].rearrange("c (r p) -> c r p", p=P),
-                position[c][:].unsqueeze(1).to_broadcast([LANES, N // P, P]),
+                position[c][:].unsqueeze(1).to_broadcast([LANES, width // P, P]),
             )
 
         for c in range(AHEAD):
@@ -76,9 +80,12 @@ def tile_bert_kernel(tc, table, pos, offs, out):
                 for d in range(WIDE, BLOCKS):
                     seed(d)
             terms = work.tile([LANES, N], F32)
-            nc.vector.tensor_tensor(
-                terms[:], window[c][:].indirect(offsets[:]), repeated[c][:], ADD
-            )
+            width = N // pieces(c)
+            for first in range(0, N, width):
+                picked = window[c][:].indirect(offsets[:, first // 16 : (first + width) // 16])
+                nc.vector.tensor_tensor(
+                    terms[:, first : first + width], picked, repeated[c][:], ADD
+                )
             total = folds.tile([LANES, T], F32)
             for k in range(K):
                 nc.tensor.matmul(

@@ -10,7 +10,6 @@ LANES = 128
 BLOCKS = C // LANES
 CHAINED = 2
 WIDE = BLOCKS - CHAINED
-AHEAD = 3
 FLOPS = C * T * (K + 1)
 
 
@@ -34,26 +33,19 @@ def tile_bert_kernel(tc, table, pos, offs, out):
         position = {}
         repeated = {}
         for c in range(BLOCKS):
+            position[c] = blocks.tile([LANES, P], F32, name="position")
+            queue = nc.scalar if c == 0 else nc.sync
+            queue.dma_start(position[c][:], pos[rows(c), :])
             window[c] = blocks.tile([LANES, V], F32, name="window")
             nc.sync.dma_start(window[c][:], table[rows(c), :])
 
-        def fetch(c):
-            position[c] = blocks.tile([LANES, P], F32, name="position")
-            nc.scalar.dma_start(position[c][:], pos[rows(c), :])
-
-        def pieces(c):
-            return 2 if c == 0 else 1
-
         def spread(c):
-            width = N // pieces(c)
-            repeated[c] = work.tile([LANES, width], F32, name="repeated")
+            repeated[c] = work.tile([LANES, N], F32, name="repeated")
             nc.scalar.copy(
                 repeated[c][:].rearrange("c (r p) -> c r p", p=P),
-                position[c][:].unsqueeze(1).to_broadcast([LANES, width // P, P]),
+                position[c][:].unsqueeze(1).to_broadcast([LANES, N // P, P]),
             )
 
-        for c in range(AHEAD):
-            fetch(c)
         spread(0)
 
         def store_mean(c, total):
@@ -72,20 +64,15 @@ def tile_bert_kernel(tc, table, pos, offs, out):
             )
 
         for c in range(WIDE):
-            if c + AHEAD < BLOCKS:
-                fetch(c + AHEAD)
             if c + 1 < WIDE:
                 spread(c + 1)
             else:
                 for d in range(WIDE, BLOCKS):
                     seed(d)
             terms = work.tile([LANES, N], F32)
-            width = N // pieces(c)
-            for first in range(0, N, width):
-                picked = window[c][:].indirect(offsets[:, first // 16 : (first + width) // 16])
-                nc.vector.tensor_tensor(
-                    terms[:, first : first + width], picked, repeated[c][:], ADD
-                )
+            nc.vector.tensor_tensor(
+                terms[:], window[c][:].indirect(offsets[:]), repeated[c][:], ADD
+            )
             total = folds.tile([LANES, T], F32)
             for k in range(K):
                 nc.tensor.matmul(

@@ -48,10 +48,12 @@ def tile_bert_kernel(tc, table, pos, offs, out):
 
         spread(0)
 
-        def store_mean(c, total):
+        def store_mean(c, total, width=T):
             mean = work.tile([LANES, T], F32)
-            nc.scalar.mul(mean[:], total[:], 1.0 / K)
-            nc.sync.dma_start(out[rows(c), :], mean[:])
+            for first in range(0, T, width):
+                columns = slice(first, first + width)
+                nc.scalar.mul(mean[:, columns], total[:, columns], 1.0 / K)
+                nc.sync.dma_start(out[rows(c), columns], mean[:, columns])
 
         running = {}
 
@@ -87,8 +89,16 @@ def tile_bert_kernel(tc, table, pos, offs, out):
         for k in range(K):
             for c in range(WIDE, BLOCKS):
                 longer = work.tile([LANES, T], F32)
-                picked = window[c][:].indirect(offsets[:, k * T // 16 : (k + 1) * T // 16])
-                nc.vector.tensor_tensor(longer[:], picked, running[c][:], ADD)
+                width = P if (k, c) == (K - 1, BLOCKS - 1) else T
+                for first in range(0, T, width):
+                    entry = k * T + first
+                    picked = window[c][:].indirect(offsets[:, entry // 16 : (entry + width) // 16])
+                    nc.vector.tensor_tensor(
+                        longer[:, first : first + width],
+                        picked,
+                        running[c][:, first : first + width],
+                        ADD,
+                    )
                 running[c] = longer
         for c in range(WIDE, BLOCKS):
-            store_mean(c, running[c])
+            store_mean(c, running[c], width=P if c == BLOCKS - 1 else T)

import concourse.mybir as mybir
from concourse.masks import make_identity

F32 = mybir.dt.float32
U16 = mybir.dt.uint16
ADD = mybir.AluOpType.add

C, V, B, P, K, T, N = 1024, 2048, 2, 128, 6, 256, 1536
LANES = 128
BLOCKS = C // LANES
CHAINED = 2
WIDE = BLOCKS - CHAINED
FLOPS = C * T * (K + 1)


def tile_bert_kernel(tc, table, pos, offs, out):
    nc = tc.nc
    with (
        tc.tile_pool(name="held", bufs=1) as held,
        tc.tile_pool(name="blocks", bufs=BLOCKS) as blocks,
        tc.tile_pool(name="work", bufs=4) as work,
        tc.psum_pool(name="folds", bufs=4) as folds,
    ):
        offsets = held.tile([LANES, N // 16], U16, name="offsets")
        nc.sync.dma_start(offsets[:], offs)
        identity = held.tile([LANES, LANES], F32, name="identity")
        make_identity(nc, identity[:])

        def rows(c):
            return slice(c * LANES, (c + 1) * LANES)

        window = {}
        position = {}
        repeated = {}
        for c in range(BLOCKS):
            position[c] = blocks.tile([LANES, P], F32, name="position")
            queue = nc.scalar if c == 0 else nc.sync
            queue.dma_start(position[c][:], pos[rows(c), :])
            window[c] = blocks.tile([LANES, V], F32, name="window")
            nc.sync.dma_start(window[c][:], table[rows(c), :])

        def spread(c):
            repeated[c] = work.tile([LANES, N], F32, name="repeated")
            nc.scalar.copy(
                repeated[c][:].rearrange("c (r p) -> c r p", p=P),
                position[c][:].unsqueeze(1).to_broadcast([LANES, N // P, P]),
            )

        spread(0)

        def store_mean(c, total, width=T):
            mean = work.tile([LANES, T], F32)
            for first in range(0, T, width):
                columns = slice(first, first + width)
                nc.scalar.mul(mean[:, columns], total[:, columns], 1.0 / K)
                nc.sync.dma_start(out[rows(c), columns], mean[:, columns])

        running = {}

        def seed(c):
            running[c] = work.tile([LANES, T], F32, name="sixfold")
            nc.scalar.mul(
                running[c][:].rearrange("c (b p) -> c b p", p=P),
                position[c][:].unsqueeze(1).to_broadcast([LANES, B, P]),
                float(K),
            )

        for c in range(WIDE):
            if c + 1 < WIDE:
                spread(c + 1)
            else:
                for d in range(WIDE, BLOCKS):
                    seed(d)
            terms = work.tile([LANES, N], F32)
            nc.vector.tensor_tensor(
                terms[:], window[c][:].indirect(offsets[:]), repeated[c][:], ADD
            )
            total = folds.tile([LANES, T], F32)
            for k in range(K):
                nc.tensor.matmul(
                    total[:],
                    identity[:],
                    terms[:, k * T : (k + 1) * T],
                    start=(k == 0),
                    stop=(k == K - 1),
                )
            store_mean(c, total)

        for k in range(K):
            for c in range(WIDE, BLOCKS):
                longer = work.tile([LANES, T], F32)
                width = P if (k, c) == (K - 1, BLOCKS - 1) else T
                for first in range(0, T, width):
                    entry = k * T + first
                    picked = window[c][:].indirect(offsets[:, entry // 16 : (entry + width) // 16])
                    nc.vector.tensor_tensor(
                        longer[:, first : first + width],
                        picked,
                        running[c][:, first : first + width],
                        ADD,
                    )
                running[c] = longer
        for c in range(WIDE, BLOCKS):
            store_mean(c, running[c], width=P if c == BLOCKS - 1 else T)
